import numpy as np
import ml_dtypes


def mxq(x, axis, fmt="e4m3"):
    dtype, down = {"e4m3": (ml_dtypes.float8_e4m3fn, 7), "e5m2": (ml_dtypes.float8_e5m2, 14)}[fmt]
    v = np.moveaxis(np.asarray(x, np.float32).astype(ml_dtypes.bfloat16).astype(np.float64), axis, -1)
    blocks = v.reshape(v.shape[:-1] + (-1, 32))
    amax = np.abs(blocks).max(-1, keepdims=True)
    byte = np.maximum(np.where(amax > 0, np.frexp(amax)[1] - 1 + 127, 0) - down, 1)
    scale = np.exp2(byte - 127.0)
    codes = (blocks / scale).astype(np.float32).astype(dtype).astype(np.float64)
    return np.moveaxis((codes * scale).reshape(v.shape), -1, axis)


WIDE = False


def mx_kscale(k):
    if not WIDE:
        return np.ones(k)
    levels = np.array([10, -10, 5, -5, 0])
    if k % 512:
        return np.exp2(np.random.permutation(np.resize(levels, k // 32))).repeat(32)
    a = np.empty((k // 512, 16))
    for p in range(k // 512):
        a[p, :8] = np.random.permutation(np.resize(levels, 8))
        for g in range(8):
            far = levels[np.abs(levels - a[p, g]) >= 10]
            a[p, g + 8] = far[np.random.randint(len(far))]
    return np.exp2(a.ravel()).repeat(32)


BF16 = ml_dtypes.bfloat16


def bf(x):
    return np.asarray(x, np.float32).astype(BF16)


def f64(x):
    return np.asarray(x).astype(np.float64)


E2M1 = np.array([0.0, 0.5, 1.0, 1.5, 2.0, 3.0, 4.0, 6.0, -0.0, -0.5, -1.0, -1.5, -2.0, -3.0, -4.0, -6.0])


def pack_weight(w, fmt):
    k, n = w.shape
    w = f64(bf(w)).reshape(k // 32, 32, n)
    amax = np.abs(w).max(1)
    if fmt == "e4m3":
        byte = np.frexp(amax)[1] - 1 + 127 - 7
    else:
        mant, ex = np.frexp(amax / 6.0)
        byte = np.where(mant > 0.5, ex, ex - 1) + 127
    byte = np.clip(np.where(amax > 0, byte, 1), 1, 254)
    scaled = (w * np.exp2(127.0 - byte)[:, None, :]).reshape(k, n).astype(np.float32)
    by_word = np.ascontiguousarray(scaled.reshape(k // 512, 128, 4, n).transpose(0, 1, 3, 2))
    if fmt == "e4m3":
        words = by_word.astype(ml_dtypes.float8_e4m3fn).view(np.uint8)
    else:
        c = by_word.astype(ml_dtypes.float4_e2m1fn).view(np.uint8) & 0xF
        words = c[..., 0::2] | (c[..., 1::2] << 4)
    return np.ascontiguousarray(words), np.ascontiguousarray(byte.astype(np.uint8).reshape(k // 512, 16, n))


def unpack_weight(words, scales, fmt):
    g, p, n, _ = words.shape
    if fmt == "e4m3":
        vals = np.ascontiguousarray(words).view(ml_dtypes.float8_e4m3fn).astype(np.float64)
    else:
        nib = np.empty((g, p, n, 4), np.uint8)
        nib[..., 0::2] = words & 0xF
        nib[..., 1::2] = words >> 4
        vals = E2M1[nib]
    vals = vals * np.repeat(np.exp2(scales.astype(np.float64) - 127.0), 8, axis=1)[..., None]
    return vals.transpose(0, 1, 3, 2).reshape(g * 512, n)


N, L, WD, C, O = 128, 64, 512, 512, 512
EPS = 1e-8
CONV_CLAMP = 256.0
ACT_GAIN = np.sqrt(2.0)
LRELU_SLOPE = 0.2
STYLE_WSCALE = 1.0 / np.sqrt(WD)
X_AMP = CONV_CLAMP / 2.0
W_AMP = np.sqrt(EPS)


def draw0():
    s, t = mx_kscale(WD), mx_kscale(C)
    x = bf(np.random.standard_normal((N, L, C)) * X_AMP)
    w = bf(np.random.standard_normal((N, WD)) * s)
    weight = bf(np.random.standard_normal((O, C)) * W_AMP / np.sqrt(C) / t[None, :])
    style_w = np.random.standard_normal((C, WD)) * t[:, None] / s[None, :]
    style_w_words, style_w_scales = pack_weight(style_w.T, "e4m3")
    return {"x": x,
            "w": w,
            "weight": weight,
            "style_w_words": style_w_words,
            "style_w_scales": style_w_scales,
            "style_b": bf((1.0 + 0.1 * np.random.standard_normal(C)) * t),
            "bias": bf(np.random.standard_normal(O) * 0.2 * X_AMP)}


def core(x, w, weight, style_w_words, style_w_scales, style_b, bias):
    wt = f64(weight)
    style = (mxq(f64(w), 1, "e4m3") @ unpack_weight(style_w_words, style_w_scales, "e4m3")) * STYLE_WSCALE + f64(style_b)
    d = mxq(np.square(style), 1, "e4m3") @ mxq(np.square(wt), 1, "e4m3").T
    decoef = 1.0 / np.sqrt(d + EPS)
    x_mod = f64(x) * style[:, None, :]
    y = mxq(x_mod, 2, "e4m3") @ mxq(wt, 1, "e4m3").T
    y = y * decoef[:, None, :]
    y = y + f64(bias)
    y = np.where(y >= 0, y, LRELU_SLOPE * y) * ACT_GAIN
    return np.clip(y, -CONV_CLAMP, CONV_CLAMP)


def e4m3fn_bytes(y):
    return np.clip(np.asarray(y, np.float64), -448.0, 448.0).astype(np.float32).astype(ml_dtypes.float8_e4m3fn).view(np.uint8)


def e4m3fn_values(b):
    return np.asarray(b, np.uint8).view(ml_dtypes.float8_e4m3fn).astype(np.float64)


def setup_inputs():
    d = draw0()
    x0 = np.asarray(d['w']).astype(np.float64)
    s = (np.max(np.abs(x0), axis=(0,), keepdims=True) / 448.0).astype(np.float32)
    out = {}
    for k, v in d.items():
        if k == 'w':
            out['w_bytes'] = e4m3fn_bytes(x0 / s.astype(np.float64))
            out['w_scale'] = s
        else:
            out[k] = v
    return out


def reference(x, w_bytes, w_scale, weight, style_w_words, style_w_scales, style_b, bias):
    return core(x, e4m3fn_values(w_bytes) * w_scale.astype(np.float64), weight, style_w_words, style_w_scales, style_b, bias)

@@ -1,0 +1,371 @@
+from contextlib import ExitStack
+import math
+
+import concourse.mybir as mybir
+from concourse.masks import make_identity
+
+F32 = mybir.dt.float32
+BF16 = mybir.dt.bfloat16
+U32 = mybir.dt.uint32
+I32 = mybir.dt.int32
+U8 = mybir.dt.uint8
+F8 = mybir.dt.float8_e4m3fn
+X4 = mybir.dt.float8_e4m3fn_x4
+ALU = mybir.AluOpType
+ACT = mybir.ActivationFunctionType
+
+N, L, WD, C, O = 128, 64, 512, 512, 512
+P = 128
+J = 2
+GT = P * J
+GROUPS = N * L // GT
+NS = GT // L
+EPS = 1e-8
+HUGE = 3.0e38
+FLOPS = 2 * N * L * C * O + 2 * N * WD * C + 2 * N * C * O
+KINDS = ["P","QS","P","QV","P","QS","P","P"]
+
+
+FIXED = {(31, 1): "VV"}
+
+
+def kind_of(g, j):
+    return FIXED.get((g, j), KINDS[(J * g + j) % len(KINDS)])
+
+
+def tile_modulatemlp_pa_w8_kernel(
+    tc, x, w_bytes, w_scale, weight, style_w_words, style_w_scales, style_b, bias, out
+):
+    nc = tc.nc
+    gain = 0.2 * math.sqrt(2.0)
+    xg = x.rearrange("n l c -> (n l) c").rearrange("(g p j) c -> g p j c", p=P, j=J)
+    og = out.rearrange("n l c -> (n l) c").rearrange("(g p j) c -> g p j c", p=P, j=J)
+
+    with ExitStack() as ctx:
+        const = ctx.enter_context(tc.tile_pool(name="const", bufs=1))
+        xmp = ctx.enter_context(tc.tile_pool(name="xmp", bufs=3))
+        ap = ctx.enter_context(tc.tile_pool(name="ap", bufs=4))
+        op = ctx.enter_context(tc.tile_pool(name="op", bufs=5))
+        psum = ctx.enter_context(tc.psum_pool(name="psum", bufs=1))
+        ctx.enter_context(tc.manual_schedule())
+
+        wb = const.tile([P, WD], U8, name="wb", align_bytes=64)
+        nc.sync.dma_start(out=wb[:], in_=w_bytes)
+        wsc = const.tile([P, 4], F32, name="wsc")
+        nc.sync.dma_start(out=wsc[:], in_=w_scale.rearrange("o (p t) -> p (o t)", t=4))
+        ssc = const.tile([P, C], U8, name="ssc", align_bytes=64)
+        nc.vector.memset(ssc[:].bitcast(U32), 0)
+        for q in range(4):
+            nc.sync.dma_start(
+                out=ssc[32 * q : 32 * q + 4, :].bitcast(I32),
+                in_=style_w_scales[0][4 * q : 4 * q + 4, :].bitcast(I32),
+            )
+        sw = const.tile([P, 4 * C], U8, name="sw", align_bytes=64)
+        nc.sync.dma_start(out=sw[:], in_=style_w_words[0].rearrange("p n t -> p (n t)"))
+        sb = const.tile([P, 4], BF16, name="sb")
+        nc.sync.dma_start(out=sb[:], in_=style_b.rearrange("(p t) -> p t", t=4))
+        wsb = const.tile([P, 4, C], BF16, name="wsb", align_bytes=64)
+        wview = weight.rearrange("(m b) c -> m b c", b=4)
+        for h in range(2):
+            nc.sync.dma_start(out=wsb[:, 2 * h : 2 * h + 2, :], in_=wview[:, 2 * h : 2 * h + 2, :])
+        xtiles = {}
+        bb = const.tile([P, 4], BF16, name="bb")
+        g0 = 0
+        for n_g in [1, 1] + [2] * ((GROUPS - 2) // 2):
+            xt = const.tile([P, n_g, J, C], BF16, name="x%d" % g0, align_bytes=64)
+            nc.sync.dma_start(out=xt[:], in_=xg[g0 : g0 + n_g].rearrange("g p j c -> p g j c"))
+            for k in range(n_g):
+                xtiles[g0 + k] = (xt, k)
+            if g0 == 1:
+                nc.sync.dma_start(out=bb[:], in_=bias.rearrange("(m b) -> m b", b=4))
+            g0 += n_g
+
+        one = const.tile([P, 1], F32, name="one")
+        nc.vector.memset(one[:], 1.0)
+        warm = const.tile([P, 1], F32, name="warm")
+        nc.scalar.activation(warm[:], one[:], ACT.Abs_reciprocal_sqrt)
+        ident = const.tile([P, P], F32, name="ident")
+        make_identity(nc, ident[:])
+
+        def transpose_words(dst, words):
+            for u in range(2):
+                nc.tensor.transpose(dst[:, u, :], words[:, u : C // 2 : 2], ident[:])
+
+        w16 = const.tile([P, WD], BF16, name="w16", align_bytes=64)
+        nc.vector.tensor_copy(out=w16[:], in_=wb[:].bitcast(F8))
+        wtp = psum.tile([P, 2, 2, P], F32, name="wtp", tag="xp", bufs=2)
+        transpose_words(wtp[:, 0], w16[:].bitcast(F32))
+
+        wt = const.tile([P, O, 4], BF16, name="wt", align_bytes=64)
+        wt32 = wt[:].rearrange("p o t -> p (o t)").bitcast(F32)
+        wc = const.tile([P, O], U32, name="wc", align_bytes=64)
+        wcs = const.tile([P, O], U8, name="wcs", align_bytes=64)
+        w2 = const.tile([P, O, 4], BF16, name="w2", align_bytes=64)
+        w2c = const.tile([P, O], U32, name="w2c", align_bytes=64)
+        w2s = const.tile([P, O], U8, name="w2s", align_bytes=64)
+        sq = const.tile([P, N, 4], BF16, name="sq", align_bytes=64)
+        sqc = const.tile([P, N], U32, name="sqc", align_bytes=64)
+        sqs = const.tile([P, N], U8, name="sqs", align_bytes=64)
+        halves = [slice(0, O // 2), slice(O // 2, O)]
+
+        def turn_weight(h):
+            ww = psum.tile([P, 2, 2, P], F32, name="ww", tag="zp", bufs=4)
+            for k in range(2):
+                transpose_words(ww[:, k], wsb[:, 2 * h + k, :].bitcast(F32))
+            nc.scalar.copy(
+                out=wt32[:, 512 * h : 512 * h + 512].rearrange("p (b r u) -> p b r u", b=2, u=2),
+                in_=ww[:].rearrange("p b u r -> p b r u"),
+            )
+
+        sscp = const.tile([P, C], U8, name="sscp", align_bytes=64)
+        nc.vector.tensor_copy(
+            out=sscp[:].rearrange("p (t m) -> p t m", t=4),
+            in_=ssc[:].rearrange("p (m t) -> p t m", t=4),
+        )
+        wm = const.tile([P, N, 4], BF16, name="wm", align_bytes=64)
+        nc.vector.tensor_tensor(
+            out=wm[:].rearrange("p n (u e) -> p n u e", u=2),
+            in0=wtp[:, 0].bitcast(BF16).rearrange("p u (n e) -> p n u e", e=2),
+            in1=wsc[:].rearrange("p (u e) -> p u e", u=2).unsqueeze(1).to_broadcast([P, N, 2, 2]),
+            op=ALU.mult,
+        )
+        swp = const.tile([P, C], I32, name="swp", align_bytes=64)
+        nc.vector.tensor_copy(
+            out=swp[:].rearrange("p (t m) -> p t m", t=4),
+            in_=sw[:].bitcast(I32).rearrange("p (m t) -> p t m", t=4),
+        )
+        wq = const.tile([P, N], U32, name="wq", align_bytes=64)
+        wqs = const.tile([P, N], U8, name="wqs", align_bytes=64)
+        nc.vector.quantize_mx(out=wq[:].bitcast(X4), scales=wqs[:], in_=wm[:].rearrange("p n t -> p (n t)"))
+        turn_weight(0)
+
+        styT = const.tile([P, 4, N], F32, name="styT", align_bytes=64)
+        sp = [
+            psum.tile([P, 2, P], F32, name="sp0", tag="ya", bufs=1),
+            psum.tile([P, 2, P], F32, name="sp1", tag="yb", bufs=1),
+        ]
+        for t in range(4):
+            nc.tensor.matmul_mx(
+                out=sp[t // 2][:, t % 2, :],
+                lhsT=swp[:, P * t : P * t + P].bitcast(X4),
+                lhsT_scale=sscp[:, P * t : P * t + P],
+                rhs=wq[:].bitcast(X4),
+                rhs_scale=wqs[:],
+                start=True,
+                stop=True,
+            )
+        wscale = 1.0 / math.sqrt(WD)
+        for t in range(2):
+            nc.scalar.activation(
+                styT[:, t, :], sp[0][:, t, :], ACT.Identity, scale=wscale, bias=sb[:, t : t + 1]
+            )
+        for t in range(2, 4):
+            nc.vector.tensor_scalar(
+                out=styT[:, t, :], in0=sp[1][:, t - 2, :], scalar1=wscale, scalar2=sb[:, t : t + 1],
+                op0=ALU.mult, op1=ALU.add,
+            )
+        turn_weight(1)
+
+        xp, xm, xq, yy, aa, cc, zz, rr, oo = {}, {}, {}, {}, {}, {}, {}, {}, {}
+
+        def stage_x(g):
+            xt, k = xtiles[g]
+            xp[g] = psum.tile([P, J, 2, P], F32, name="xpt", tag="xp", bufs=2)
+            for j in range(J):
+                transpose_words(xp[g][:, j], xt[:, k, j, :].bitcast(F32))
+
+        def stage_a(g, j):
+            if j == 0:
+                xm[g] = xmp.tile([P, J, P, 4], BF16, name="xm", align_bytes=64)
+            nc.vector.tensor_tensor(
+                out=xm[g][:, j].rearrange("p (n i) (u e) -> p n i u e", n=NS, u=2),
+                in0=xp[g][:, j].bitcast(BF16).rearrange("p u (n i e) -> p n i u e", n=NS, e=2),
+                in1=styT[:, :, NS * g : NS * g + NS]
+                .rearrange("p (u e) n -> p n u e", u=2)
+                .unsqueeze(2)
+                .to_broadcast([P, NS, P // NS, 2, 2]),
+                op=ALU.mult,
+            )
+
+        def stage_b(g):
+            xc = xmp.tile([P, GT], U32, name="xc", align_bytes=64)
+            xs = xmp.tile([P, GT], U8, name="xs", align_bytes=64)
+            nc.vector.quantize_mx(
+                out=xc[:].bitcast(X4), scales=xs[:], in_=xm.pop(g)[:].rearrange("p j r t -> p (j r t)")
+            )
+            xq[g] = (xc, xs)
+
+        def stage_m(g):
+            xc, xs = xq.pop(g)
+            for h in range(2):
+                y = psum.tile([P, 2, GT], F32, name="y%d" % h, tag="ya" if h == 0 else "yb", bufs=1)
+                for k in range(2):
+                    ob = 2 * h + k
+                    nc.tensor.matmul_mx(
+                        out=y[:, k, :],
+                        lhsT=wc[:, P * ob : P * ob + P].bitcast(X4),
+                        lhsT_scale=wcs[:, P * ob : P * ob + P],
+                        rhs=xc[:].bitcast(X4),
+                        rhs_scale=xs[:],
+                        start=True,
+                        stop=True,
+                    )
+                yy[g, h] = y
+
+        def stage_e(g, h, on_vector=False):
+            if h == 0:
+                aa[g] = ap.tile([P, 4, GT], F32, name="a")
+            y = yy.pop((g, h))
+            for k in range(2):
+                ob = 2 * h + k
+                yv = y[:, k, :].rearrange("p (j n i) -> p n j i", j=J, n=NS)
+                av = aa[g][:, ob, :].rearrange("p (j n i) -> p n j i", j=J, n=NS)
+                for n in range(NS):
+                    s = NS * g + n
+                    if on_vector:
+                        nc.vector.tensor_scalar(
+                            out=av[:, n], in0=yv[:, n], scalar1=dT[:, ob, s : s + 1], scalar2=bT[:, ob : ob + 1],
+                            op0=ALU.mult, op1=ALU.add,
+                        )
+                    else:
+                        nc.scalar.activation(
+                            av[:, n], yv[:, n], ACT.Identity, scale=dT[:, ob, s : s + 1], bias=bT[:, ob : ob + 1]
+                        )
+
+        def stage_q(g):
+            for j in range(J):
+                if kind_of(g, j) == "VV":
+                    cc[g, j] = ap.tile([P, 4, P], F32, name="c")
+                    nc.vector.tensor_scalar(
+                        out=cc[g, j][:], in0=aa[g][:, :, P * j : P * j + P], scalar1=0.0, scalar2=4.0,
+                        op0=ALU.max, op1=ALU.mult,
+                    )
+                elif kind_of(g, j) != "P":
+                    c = ap.tile([P, 4, P], F32, name="c")
+                    nc.gpsimd.tensor_scalar(
+                        out=c[:], in0=aa[g][:, :, P * j : P * j + P], scalar1=HUGE, scalar2=0.0,
+                        op0=ALU.min, op1=ALU.max,
+                    )
+                    nc.gpsimd.tensor_scalar(
+                        out=c[:], in0=c[:], scalar1=4.0, scalar2=1.0, op0=ALU.mult, op1=ALU.mult
+                    )
+                    cc[g, j] = c
+
+        def stage_z(g, j):
+            if True:
+                z = psum.tile([P, O], F32, name="z", tag="zp", bufs=4)
+                for ob in range(4):
+                    dst = z[:, P * ob : P * ob + P]
+                    src = aa[g][:, ob, P * j : P * j + P]
+                    if kind_of(g, j) == "P":
+                        nc.tensor.transpose(dst, src, ident[:])
+                    else:
+                        nc.tensor.matmul(dst, lhsT=src, rhs=ident[:], start=True, stop=False, is_transpose=True)
+                        nc.tensor.matmul(
+                            dst, lhsT=cc[g, j][:, ob, :], rhs=ident[:], start=False, stop=True, is_transpose=True
+                        )
+                zz[g, j] = z
+
+        def out_view(g, j):
+            if g not in oo:
+                oo[g] = op.tile([P, J, O], F32, name="o")
+            return oo[g][:, j, :].rearrange("p (m b) -> p m b", b=4)
+
+        def z_view(g, j):
+            return zz[g, j][:].rearrange("p (b m) -> p m b", b=4)
+
+        def stage_c(g, j):
+            if kind_of(g, j) == "QS":
+                nc.scalar.copy(out=out_view(g, j), in_=z_view(g, j))
+            if kind_of(g, j) == "P":
+                rr[g, j] = ap.tile([P, O], F32, name="r", bufs=4)
+                nc.scalar.copy(out=rr[g, j][:].rearrange("p (m b) -> p m b", b=4), in_=z_view(g, j))
+
+        def stage_l(g, j):
+            if kind_of(g, j) in ("QV", "VV"):
+                nc.vector.tensor_scalar(
+                    out=out_view(g, j), in0=z_view(g, j), scalar1=256.0, scalar2=-256.0, op0=ALU.min, op1=ALU.max
+                )
+            if kind_of(g, j) == "P":
+                nc.vector.scalar_tensor_tensor(
+                    out=out_view(g, j),
+                    in0=z_view(g, j),
+                    scalar=5.0,
+                    in1=rr.pop((g, j))[:].rearrange("p (m b) -> p m b", b=4),
+                    op0=ALU.mult,
+                    op1=ALU.max,
+                )
+
+        def stage_k(g, j):
+            if kind_of(g, j) in ("P", "QS"):
+                ov = oo[g][:, j, :]
+                eng = nc.vector if g == GROUPS - 1 else nc.gpsimd
+                eng.tensor_scalar(out=ov, in0=ov, scalar1=256.0, scalar2=-256.0, op0=ALU.min, op1=ALU.max)
+
+        def stage_o(g):
+            nc.sync.dma_start(out=og[g], in_=oo.pop(g)[:])
+
+        stage_x(0)
+        stage_x(1)
+        nc.gpsimd.tensor_tensor(out=w2[:, halves[0], :], in0=wt[:, halves[0], :], in1=wt[:, halves[0], :], op=ALU.mult)
+        nc.scalar.activation(w2[:, halves[1], :], wt[:, halves[1], :], ACT.Square)
+        nc.scalar.activation(sq[:], styT[:].rearrange("p t n -> p n t"), ACT.Square)
+        stage_a(0, 0)
+        nc.vector.quantize_mx(out=wc[:].bitcast(X4), scales=wcs[:], in_=wt[:].rearrange("p o t -> p (o t)"))
+        stage_a(0, 1)
+        nc.vector.quantize_mx(out=w2c[:].bitcast(X4), scales=w2s[:], in_=w2[:].rearrange("p o t -> p (o t)"))
+        nc.vector.quantize_mx(out=sqc[:].bitcast(X4), scales=sqs[:], in_=sq[:].rearrange("p n t -> p (n t)"))
+        stage_b(0)
+        dp = psum.tile([P, 4, N], F32, name="dp", tag="zp", bufs=4)
+        for ob in range(4):
+            nc.tensor.matmul_mx(
+                out=dp[:, ob, :],
+                lhsT=w2c[:, P * ob : P * ob + P].bitcast(X4),
+                lhsT_scale=w2s[:, P * ob : P * ob + P],
+                rhs=sqc[:].bitcast(X4),
+                rhs_scale=sqs[:],
+                start=True,
+                stop=True,
+            )
+        bT = const.tile([P, 4], F32, name="bT")
+        nc.vector.tensor_scalar(out=bT[:], in0=bb[:], scalar1=gain, scalar2=None, op0=ALU.mult)
+        dT = const.tile([P, 4, N], F32, name="dT")
+        nc.scalar.activation(
+            dT[:], dp[:], ACT.Abs_reciprocal_sqrt, scale=1.0 / gain**2, bias=EPS / gain**2
+        )
+
+        def has(g):
+            return 0 <= g < GROUPS
+
+        for i in range(GROUPS + 4):
+            if has(i):
+                stage_m(i)
+            if has(i + 2):
+                stage_x(i + 2)
+            if has(i - 1):
+                stage_z(i - 1, 0)
+            if has(i - 2):
+                stage_z(i - 2, 1)
+            if has(i):
+                stage_e(i, 0)
+                stage_e(i, 1, on_vector=i == GROUPS - 1)
+            if has(i - 1):
+                stage_c(i - 1, 0)
+            if has(i - 2):
+                stage_c(i - 2, 1)
+            if has(i + 1):
+                stage_a(i + 1, 0)
+                stage_a(i + 1, 1)
+            if has(i - 2):
+                stage_l(i - 2, 0)
+            if has(i + 1):
+                stage_b(i + 1)
+            if has(i - 3):
+                stage_l(i - 3, 1)
+            if has(i - 1):
+                stage_q(i - 1)
+            if has(i - 2):
+                stage_k(i - 2, 0)
+            if has(i - 3):
+                stage_k(i - 3, 1)
+                stage_o(i - 3)

@@ -23,10 +23,10 @@ NS = GT // L
 EPS = 1e-8
 HUGE = 3.0e38
 FLOPS = 2 * N * L * C * O + 2 * N * WD * C + 2 * N * C * O
-KINDS = ["P","QS","P","QV","P","QS","P","P"]
+KINDS = ["P"]
 
 
-FIXED = {(31, 1): "VV"}
+FIXED = {}
 
 
 def kind_of(g, j):

from contextlib import ExitStack
import math

import concourse.mybir as mybir
from concourse.masks import make_identity

F32 = mybir.dt.float32
BF16 = mybir.dt.bfloat16
U32 = mybir.dt.uint32
I32 = mybir.dt.int32
U8 = mybir.dt.uint8
F8 = mybir.dt.float8_e4m3fn
X4 = mybir.dt.float8_e4m3fn_x4
ALU = mybir.AluOpType
ACT = mybir.ActivationFunctionType

N, L, WD, C, O = 128, 64, 512, 512, 512
P = 128
J = 2
GT = P * J
GROUPS = N * L // GT
NS = GT // L
EPS = 1e-8
HUGE = 3.0e38
FLOPS = 2 * N * L * C * O + 2 * N * WD * C + 2 * N * C * O
KINDS = ["P"]


FIXED = {}


def kind_of(g, j):
    return FIXED.get((g, j), KINDS[(J * g + j) % len(KINDS)])


def tile_modulatemlp_pa_w8_kernel(
    tc, x, w_bytes, w_scale, weight, style_w_words, style_w_scales, style_b, bias, out
):
    nc = tc.nc
    gain = 0.2 * math.sqrt(2.0)
    xg = x.rearrange("n l c -> (n l) c").rearrange("(g p j) c -> g p j c", p=P, j=J)
    og = out.rearrange("n l c -> (n l) c").rearrange("(g p j) c -> g p j c", p=P, j=J)

    with ExitStack() as ctx:
        const = ctx.enter_context(tc.tile_pool(name="const", bufs=1))
        xmp = ctx.enter_context(tc.tile_pool(name="xmp", bufs=3))
        ap = ctx.enter_context(tc.tile_pool(name="ap", bufs=4))
        op = ctx.enter_context(tc.tile_pool(name="op", bufs=5))
        psum = ctx.enter_context(tc.psum_pool(name="psum", bufs=1))
        ctx.enter_context(tc.manual_schedule())

        wb = const.tile([P, WD], U8, name="wb", align_bytes=64)
        nc.sync.dma_start(out=wb[:], in_=w_bytes)
        wsc = const.tile([P, 4], F32, name="wsc")
        nc.sync.dma_start(out=wsc[:], in_=w_scale.rearrange("o (p t) -> p (o t)", t=4))
        ssc = const.tile([P, C], U8, name="ssc", align_bytes=64)
        nc.vector.memset(ssc[:].bitcast(U32), 0)
        for q in range(4):
            nc.sync.dma_start(
                out=ssc[32 * q : 32 * q + 4, :].bitcast(I32),
                in_=style_w_scales[0][4 * q : 4 * q + 4, :].bitcast(I32),
            )
        sw = const.tile([P, 4 * C], U8, name="sw", align_bytes=64)
        nc.sync.dma_start(out=sw[:], in_=style_w_words[0].rearrange("p n t -> p (n t)"))
        sb = const.tile([P, 4], BF16, name="sb")
        nc.sync.dma_start(out=sb[:], in_=style_b.rearrange("(p t) -> p t", t=4))
        wsb = const.tile([P, 4, C], BF16, name="wsb", align_bytes=64)
        wview = weight.rearrange("(m b) c -> m b c", b=4)
        for h in range(2):
            nc.sync.dma_start(out=wsb[:, 2 * h : 2 * h + 2, :], in_=wview[:, 2 * h : 2 * h + 2, :])
        xtiles = {}
        bb = const.tile([P, 4], BF16, name="bb")
        g0 = 0
        for n_g in [1, 1] + [2] * ((GROUPS - 2) // 2):
            xt = const.tile([P, n_g, J, C], BF16, name="x%d" % g0, align_bytes=64)
            nc.sync.dma_start(out=xt[:], in_=xg[g0 : g0 + n_g].rearrange("g p j c -> p g j c"))
            for k in range(n_g):
                xtiles[g0 + k] = (xt, k)
            if g0 == 1:
                nc.sync.dma_start(out=bb[:], in_=bias.rearrange("(m b) -> m b", b=4))
            g0 += n_g

        one = const.tile([P, 1], F32, name="one")
        nc.vector.memset(one[:], 1.0)
        warm = const.tile([P, 1], F32, name="warm")
        nc.scalar.activation(warm[:], one[:], ACT.Abs_reciprocal_sqrt)
        ident = const.tile([P, P], F32, name="ident")
        make_identity(nc, ident[:])

        def transpose_words(dst, words):
            for u in range(2):
                nc.tensor.transpose(dst[:, u, :], words[:, u : C // 2 : 2], ident[:])

        w16 = const.tile([P, WD], BF16, name="w16", align_bytes=64)
        nc.vector.tensor_copy(out=w16[:], in_=wb[:].bitcast(F8))
        wtp = psum.tile([P, 2, 2, P], F32, name="wtp", tag="xp", bufs=2)
        transpose_words(wtp[:, 0], w16[:].bitcast(F32))

        wt = const.tile([P, O, 4], BF16, name="wt", align_bytes=64)
        wt32 = wt[:].rearrange("p o t -> p (o t)").bitcast(F32)
        wc = const.tile([P, O], U32, name="wc", align_bytes=64)
        wcs = const.tile([P, O], U8, name="wcs", align_bytes=64)
        w2 = const.tile([P, O, 4], BF16, name="w2", align_bytes=64)
        w2c = const.tile([P, O], U32, name="w2c", align_bytes=64)
        w2s = const.tile([P, O], U8, name="w2s", align_bytes=64)
        sq = const.tile([P, N, 4], BF16, name="sq", align_bytes=64)
        sqc = const.tile([P, N], U32, name="sqc", align_bytes=64)
        sqs = const.tile([P, N], U8, name="sqs", align_bytes=64)
        halves = [slice(0, O // 2), slice(O // 2, O)]

        def turn_weight(h):
            ww = psum.tile([P, 2, 2, P], F32, name="ww", tag="zp", bufs=4)
            for k in range(2):
                transpose_words(ww[:, k], wsb[:, 2 * h + k, :].bitcast(F32))
            nc.scalar.copy(
                out=wt32[:, 512 * h : 512 * h + 512].rearrange("p (b r u) -> p b r u", b=2, u=2),
                in_=ww[:].rearrange("p b u r -> p b r u"),
            )

        sscp = const.tile([P, C], U8, name="sscp", align_bytes=64)
        nc.vector.tensor_copy(
            out=sscp[:].rearrange("p (t m) -> p t m", t=4),
            in_=ssc[:].rearrange("p (m t) -> p t m", t=4),
        )
        wm = const.tile([P, N, 4], BF16, name="wm", align_bytes=64)
        nc.vector.tensor_tensor(
            out=wm[:].rearrange("p n (u e) -> p n u e", u=2),
            in0=wtp[:, 0].bitcast(BF16).rearrange("p u (n e) -> p n u e", e=2),
            in1=wsc[:].rearrange("p (u e) -> p u e", u=2).unsqueeze(1).to_broadcast([P, N, 2, 2]),
            op=ALU.mult,
        )
        swp = const.tile([P, C], I32, name="swp", align_bytes=64)
        nc.vector.tensor_copy(
            out=swp[:].rearrange("p (t m) -> p t m", t=4),
            in_=sw[:].bitcast(I32).rearrange("p (m t) -> p t m", t=4),
        )
        wq = const.tile([P, N], U32, name="wq", align_bytes=64)
        wqs = const.tile([P, N], U8, name="wqs", align_bytes=64)
        nc.vector.quantize_mx(out=wq[:].bitcast(X4), scales=wqs[:], in_=wm[:].rearrange("p n t -> p (n t)"))
        turn_weight(0)

        styT = const.tile([P, 4, N], F32, name="styT", align_bytes=64)
        sp = [
            psum.tile([P, 2, P], F32, name="sp0", tag="ya", bufs=1),
            psum.tile([P, 2, P], F32, name="sp1", tag="yb", bufs=1),
        ]
        for t in range(4):
            nc.tensor.matmul_mx(
                out=sp[t // 2][:, t % 2, :],
                lhsT=swp[:, P * t : P * t + P].bitcast(X4),
                lhsT_scale=sscp[:, P * t : P * t + P],
                rhs=wq[:].bitcast(X4),
                rhs_scale=wqs[:],
                start=True,
                stop=True,
            )
        wscale = 1.0 / math.sqrt(WD)
        for t in range(2):
            nc.scalar.activation(
                styT[:, t, :], sp[0][:, t, :], ACT.Identity, scale=wscale, bias=sb[:, t : t + 1]
            )
        for t in range(2, 4):
            nc.vector.tensor_scalar(
                out=styT[:, t, :], in0=sp[1][:, t - 2, :], scalar1=wscale, scalar2=sb[:, t : t + 1],
                op0=ALU.mult, op1=ALU.add,
            )
        turn_weight(1)

        xp, xm, xq, yy, aa, cc, zz, rr, oo = {}, {}, {}, {}, {}, {}, {}, {}, {}

        def stage_x(g):
            xt, k = xtiles[g]
            xp[g] = psum.tile([P, J, 2, P], F32, name="xpt", tag="xp", bufs=2)
            for j in range(J):
                transpose_words(xp[g][:, j], xt[:, k, j, :].bitcast(F32))

        def stage_a(g, j):
            if j == 0:
                xm[g] = xmp.tile([P, J, P, 4], BF16, name="xm", align_bytes=64)
            nc.vector.tensor_tensor(
                out=xm[g][:, j].rearrange("p (n i) (u e) -> p n i u e", n=NS, u=2),
                in0=xp[g][:, j].bitcast(BF16).rearrange("p u (n i e) -> p n i u e", n=NS, e=2),
                in1=styT[:, :, NS * g : NS * g + NS]
                .rearrange("p (u e) n -> p n u e", u=2)
                .unsqueeze(2)
                .to_broadcast([P, NS, P // NS, 2, 2]),
                op=ALU.mult,
            )

        def stage_b(g):
            xc = xmp.tile([P, GT], U32, name="xc", align_bytes=64)
            xs = xmp.tile([P, GT], U8, name="xs", align_bytes=64)
            nc.vector.quantize_mx(
                out=xc[:].bitcast(X4), scales=xs[:], in_=xm.pop(g)[:].rearrange("p j r t -> p (j r t)")
            )
            xq[g] = (xc, xs)

        def stage_m(g):
            xc, xs = xq.pop(g)
            for h in range(2):
                y = psum.tile([P, 2, GT], F32, name="y%d" % h, tag="ya" if h == 0 else "yb", bufs=1)
                for k in range(2):
                    ob = 2 * h + k
                    nc.tensor.matmul_mx(
                        out=y[:, k, :],
                        lhsT=wc[:, P * ob : P * ob + P].bitcast(X4),
                        lhsT_scale=wcs[:, P * ob : P * ob + P],
                        rhs=xc[:].bitcast(X4),
                        rhs_scale=xs[:],
                        start=True,
                        stop=True,
                    )
                yy[g, h] = y

        def stage_e(g, h, on_vector=False):
            if h == 0:
                aa[g] = ap.tile([P, 4, GT], F32, name="a")
            y = yy.pop((g, h))
            for k in range(2):
                ob = 2 * h + k
                yv = y[:, k, :].rearrange("p (j n i) -> p n j i", j=J, n=NS)
                av = aa[g][:, ob, :].rearrange("p (j n i) -> p n j i", j=J, n=NS)
                for n in range(NS):
                    s = NS * g + n
                    if on_vector:
                        nc.vector.tensor_scalar(
                            out=av[:, n], in0=yv[:, n], scalar1=dT[:, ob, s : s + 1], scalar2=bT[:, ob : ob + 1],
                            op0=ALU.mult, op1=ALU.add,
                        )
                    else:
                        nc.scalar.activation(
                            av[:, n], yv[:, n], ACT.Identity, scale=dT[:, ob, s : s + 1], bias=bT[:, ob : ob + 1]
                        )

        def stage_q(g):
            for j in range(J):
                if kind_of(g, j) == "VV":
                    cc[g, j] = ap.tile([P, 4, P], F32, name="c")
                    nc.vector.tensor_scalar(
                        out=cc[g, j][:], in0=aa[g][:, :, P * j : P * j + P], scalar1=0.0, scalar2=4.0,
                        op0=ALU.max, op1=ALU.mult,
                    )
                elif kind_of(g, j) != "P":
                    c = ap.tile([P, 4, P], F32, name="c")
                    nc.gpsimd.tensor_scalar(
                        out=c[:], in0=aa[g][:, :, P * j : P * j + P], scalar1=HUGE, scalar2=0.0,
                        op0=ALU.min, op1=ALU.max,
                    )
                    nc.gpsimd.tensor_scalar(
                        out=c[:], in0=c[:], scalar1=4.0, scalar2=1.0, op0=ALU.mult, op1=ALU.mult
                    )
                    cc[g, j] = c

        def stage_z(g, j):
            if True:
                z = psum.tile([P, O], F32, name="z", tag="zp", bufs=4)
                for ob in range(4):
                    dst = z[:, P * ob : P * ob + P]
                    src = aa[g][:, ob, P * j : P * j + P]
                    if kind_of(g, j) == "P":
                        nc.tensor.transpose(dst, src, ident[:])
                    else:
                        nc.tensor.matmul(dst, lhsT=src, rhs=ident[:], start=True, stop=False, is_transpose=True)
                        nc.tensor.matmul(
                            dst, lhsT=cc[g, j][:, ob, :], rhs=ident[:], start=False, stop=True, is_transpose=True
                        )
                zz[g, j] = z

        def out_view(g, j):
            if g not in oo:
                oo[g] = op.tile([P, J, O], F32, name="o")
            return oo[g][:, j, :].rearrange("p (m b) -> p m b", b=4)

        def z_view(g, j):
            return zz[g, j][:].rearrange("p (b m) -> p m b", b=4)

        def stage_c(g, j):
            if kind_of(g, j) == "QS":
                nc.scalar.copy(out=out_view(g, j), in_=z_view(g, j))
            if kind_of(g, j) == "P":
                rr[g, j] = ap.tile([P, O], F32, name="r", bufs=4)
                nc.scalar.copy(out=rr[g, j][:].rearrange("p (m b) -> p m b", b=4), in_=z_view(g, j))

        def stage_l(g, j):
            if kind_of(g, j) in ("QV", "VV"):
                nc.vector.tensor_scalar(
                    out=out_view(g, j), in0=z_view(g, j), scalar1=256.0, scalar2=-256.0, op0=ALU.min, op1=ALU.max
                )
            if kind_of(g, j) == "P":
                nc.vector.scalar_tensor_tensor(
                    out=out_view(g, j),
                    in0=z_view(g, j),
                    scalar=5.0,
                    in1=rr.pop((g, j))[:].rearrange("p (m b) -> p m b", b=4),
                    op0=ALU.mult,
                    op1=ALU.max,
                )

        def stage_k(g, j):
            if kind_of(g, j) in ("P", "QS"):
                ov = oo[g][:, j, :]
                eng = nc.vector if g == GROUPS - 1 else nc.gpsimd
                eng.tensor_scalar(out=ov, in0=ov, scalar1=256.0, scalar2=-256.0, op0=ALU.min, op1=ALU.max)

        def stage_o(g):
            nc.sync.dma_start(out=og[g], in_=oo.pop(g)[:])

        stage_x(0)
        stage_x(1)
        nc.gpsimd.tensor_tensor(out=w2[:, halves[0], :], in0=wt[:, halves[0], :], in1=wt[:, halves[0], :], op=ALU.mult)
        nc.scalar.activation(w2[:, halves[1], :], wt[:, halves[1], :], ACT.Square)
        nc.scalar.activation(sq[:], styT[:].rearrange("p t n -> p n t"), ACT.Square)
        stage_a(0, 0)
        nc.vector.quantize_mx(out=wc[:].bitcast(X4), scales=wcs[:], in_=wt[:].rearrange("p o t -> p (o t)"))
        stage_a(0, 1)
        nc.vector.quantize_mx(out=w2c[:].bitcast(X4), scales=w2s[:], in_=w2[:].rearrange("p o t -> p (o t)"))
        nc.vector.quantize_mx(out=sqc[:].bitcast(X4), scales=sqs[:], in_=sq[:].rearrange("p n t -> p (n t)"))
        stage_b(0)
        dp = psum.tile([P, 4, N], F32, name="dp", tag="zp", bufs=4)
        for ob in range(4):
            nc.tensor.matmul_mx(
                out=dp[:, ob, :],
                lhsT=w2c[:, P * ob : P * ob + P].bitcast(X4),
                lhsT_scale=w2s[:, P * ob : P * ob + P],
                rhs=sqc[:].bitcast(X4),
                rhs_scale=sqs[:],
                start=True,
                stop=True,
            )
        bT = const.tile([P, 4], F32, name="bT")
        nc.vector.tensor_scalar(out=bT[:], in0=bb[:], scalar1=gain, scalar2=None, op0=ALU.mult)
        dT = const.tile([P, 4, N], F32, name="dT")
        nc.scalar.activation(
            dT[:], dp[:], ACT.Abs_reciprocal_sqrt, scale=1.0 / gain**2, bias=EPS / gain**2
        )

        def has(g):
            return 0 <= g < GROUPS

        for i in range(GROUPS + 4):
            if has(i):
                stage_m(i)
            if has(i + 2):
                stage_x(i + 2)
            if has(i - 1):
                stage_z(i - 1, 0)
            if has(i - 2):
                stage_z(i - 2, 1)
            if has(i):
                stage_e(i, 0)
                stage_e(i, 1, on_vector=i == GROUPS - 1)
            if has(i - 1):
                stage_c(i - 1, 0)
            if has(i - 2):
                stage_c(i - 2, 1)
            if has(i + 1):
                stage_a(i + 1, 0)
                stage_a(i + 1, 1)
            if has(i - 2):
                stage_l(i - 2, 0)
            if has(i + 1):
                stage_b(i + 1)
            if has(i - 3):
                stage_l(i - 3, 1)
            if has(i - 1):
                stage_q(i - 1)
            if has(i - 2):
                stage_k(i - 2, 0)
            if has(i - 3):
                stage_k(i - 3, 1)
                stage_o(i - 3)
